import numpy as np
import ml_dtypes


def mxq(x, axis, fmt="e4m3"):
    dtype, down = {"e4m3": (ml_dtypes.float8_e4m3fn, 7), "e5m2": (ml_dtypes.float8_e5m2, 14)}[fmt]
    v = np.moveaxis(np.asarray(x, np.float32).astype(ml_dtypes.bfloat16).astype(np.float64), axis, -1)
    blocks = v.reshape(v.shape[:-1] + (-1, 32))
    amax = np.abs(blocks).max(-1, keepdims=True)
    byte = np.maximum(np.where(amax > 0, np.frexp(amax)[1] - 1 + 127, 0) - down, 1)
    scale = np.exp2(byte - 127.0)
    codes = (blocks / scale).astype(np.float32).astype(dtype).astype(np.float64)
    return np.moveaxis((codes * scale).reshape(v.shape), -1, axis)


WIDE = False


def mx_kscale(k):
    if not WIDE:
        return np.ones(k)
    levels = np.array([20, -20, 10, -10, 0])
    a = np.random.permutation(np.resize(levels, k // 512 * 4)).reshape(k // 512, 4)
    idx = np.arange(k)
    return np.exp2(a[idx // 512, idx % 128 // 32])


BF16 = ml_dtypes.bfloat16


def bf(x):
    return np.asarray(x, np.float32).astype(BF16)


def f64(x):
    return np.asarray(x).astype(np.float64)


B, S, IN, OUT = 2, 2048, 256, 128


def _hamilton_weight(r, i, j, k):
    col0 = np.concatenate([r, -i, -j, -k], axis=0)
    col1 = np.concatenate([i, r, -k, j], axis=0)
    col2 = np.concatenate([j, k, r, -i], axis=0)
    col3 = np.concatenate([k, -j, i, r], axis=0)
    return np.concatenate([col0, col1, col2, col3], axis=1)


def setup_inputs():
    u = mx_kscale(4 * OUT)[:OUT]
    sc = 1.0 / np.sqrt(2 * IN)
    x = np.random.standard_normal((B, S, 4 * IN))
    r = np.random.standard_normal((IN, OUT)) * sc / u[None, :]
    i = np.random.standard_normal((IN, OUT)) * sc / u[None, :]
    j = np.random.standard_normal((IN, OUT)) * sc / u[None, :]
    k = np.random.standard_normal((IN, OUT)) * sc / u[None, :]
    b = np.random.standard_normal(4 * OUT) * 0.5
    g = np.random.standard_normal((B, S, 4 * OUT)) * np.exp2(np.random.randint(-12, 1, (B, S, 1))) * 8.0 * np.tile(u, 4)
    return {"x": bf(x), "r_weight": bf(r), "i_weight": bf(i), "j_weight": bf(j), "k_weight": bf(k),
            "bias": bf(b), "grad_out": bf(g)}


def reference(x, r_weight, i_weight, j_weight, k_weight, bias, grad_out):
    wq = mxq(np.concatenate([f64(r_weight), f64(i_weight), f64(j_weight), f64(k_weight)], axis=1), 1, "e4m3")
    rq, iq, jq, kq = wq[:, :OUT], wq[:, OUT:2 * OUT], wq[:, 2 * OUT:3 * OUT], wq[:, 3 * OUT:]
    W = _hamilton_weight(rq, iq, jq, kq)
    return mxq(f64(grad_out), 2, "e5m2") @ W.T

@@ -1,0 +1,175 @@
+from contextlib import ExitStack
+
+import concourse.masks as masks
+import concourse.mybir as mybir
+
+F32 = mybir.dt.float32
+BF16 = mybir.dt.bfloat16
+U32 = mybir.dt.uint32
+U8 = mybir.dt.uint8
+E4M3X4 = mybir.dt.float8_e4m3fn_x4
+E5M2X4 = mybir.dt.float8_e5m2_x4
+
+P = 128
+TOKENS = 4096
+K = 512
+N = 1024
+TILES = TOKENS // P
+BANK = 512
+
+FLOPS = 2 * TOKENS * K * N
+BYTES = TOKENS * K * 2 + 4 * 256 * 128 * 2 + TOKENS * N * 4
+
+HAMILTON = (
+    ((0, 1.0), (1, 1.0), (2, 1.0), (3, 1.0)),
+    ((1, -1.0), (0, 1.0), (3, 1.0), (2, -1.0)),
+    ((2, -1.0), (3, -1.0), (0, 1.0), (1, 1.0)),
+    ((3, -1.0), (2, 1.0), (1, -1.0), (0, 1.0)),
+)
+
+LOAD_TILES = (2, 2, 4, 8, 8, 8)
+GROUP_TILES = (2, 2, 4, 4, 4, 4, 4, 4, 4)
+
+
+def tile_qlinear_t_kernel(
+    tc, x, r_weight, i_weight, j_weight, k_weight, bias, grad_out, out
+):
+    nc = tc.nc
+    assert sum(LOAD_TILES) == TILES and sum(GROUP_TILES) == TILES
+    g_dram = grad_out.flatten_outer_dims().rearrange("(p a) k -> p a k", a=TILES)
+    out_dram = out.flatten_outer_dims().rearrange("(p a) n -> p a n", a=TILES)
+
+    with ExitStack() as ctx:
+        keep = ctx.enter_context(tc.tile_pool(name="keep", bufs=1))
+        ring = ctx.enter_context(tc.tile_pool(name="ring", bufs=3))
+        psum = ctx.enter_context(tc.psum_pool(name="psum", bufs=8))
+
+        w_rows = [keep.tile([P, 2, K], BF16, name="w_rows%d" % rb) for rb in range(4)]
+        for c, w in enumerate((r_weight, i_weight, j_weight, k_weight)):
+            nc.sync.dma_start(
+                out=w_rows[0][:, :, c * P : (c + 1) * P],
+                in_=w.rearrange("(a p) k -> p a k", p=P),
+            )
+        g_rows = []
+        first = 0
+        for c, count in enumerate(LOAD_TILES):
+            chunk = keep.tile([P, count, K], BF16, name="g_chunk%d" % c)
+            nc.sync.dma_start(out=chunk[:], in_=g_dram[:, first : first + count, :])
+            g_rows.extend([chunk[:, a, :] for a in range(count)])
+            first += count
+
+        ident = keep.tile([P, P], F32, name="ident")
+        masks.make_identity(nc, ident[:])
+
+        for rb in range(1, 4):
+            c = 0
+            while c < 4:
+                src, sign = HAMILTON[rb][c]
+                run = 1
+                while c + run < 4 and HAMILTON[rb][c + run] == (src + run, sign):
+                    run += 1
+                dst_ap = w_rows[rb][:, :, c * P : (c + run) * P]
+                src_ap = w_rows[0][:, :, src * P : (src + run) * P]
+                if sign > 0:
+                    nc.vector.tensor_copy(out=dst_ap, in_=src_ap)
+                else:
+                    nc.vector.tensor_scalar_mul(out=dst_ap, in0=src_ap, scalar1=-1.0)
+                c += run
+
+        def transpose_pair(rows_pair, grouped_words, on_vector):
+            bank = psum.tile([P, BANK], F32, name="bank", tag="bank")
+            planes = bank[:].rearrange("p (a u j) -> p a u j", a=2, u=2)
+            for a, rows in enumerate(rows_pair):
+                words = rows.bitcast(F32).rearrange("p (w u) -> p u w", u=2)
+                for u in range(2):
+                    nc.tensor.transpose(planes[:, a, u, :], words[:, u, :], ident[:])
+            dst_ap = grouped_words.rearrange("p (a j u) -> p a j u", a=2, u=2)
+            src_ap = bank[:].rearrange("p (a u j) -> p a j u", a=2, u=2)
+            if on_vector:
+                nc.vector.tensor_copy(out=dst_ap, in_=src_ap)
+            else:
+                nc.scalar.copy(out=dst_ap, in_=src_ap)
+
+        w_grouped = keep.tile([P, 4 * N], BF16, name="w_grouped", align_bytes=64)
+        w_codes = keep.tile([P, N], U32, name="w_codes", align_bytes=64)
+        w_scales = keep.tile([P, N], U8, name="w_scales", align_bytes=64)
+
+        def prepare_w(half):
+            for rb in (2 * half, 2 * half + 1):
+                transpose_pair(
+                    (w_rows[rb][:, 0, :], w_rows[rb][:, 1, :]),
+                    w_grouped[:].bitcast(F32)[:, rb * BANK : (rb + 1) * BANK],
+                    rb % 2 == 1,
+                )
+
+        def quantise_w(half):
+            nc.vector.quantize_mx(
+                out=w_codes[:, half * BANK : (half + 1) * BANK].bitcast(E4M3X4),
+                scales=w_scales[:, half * BANK : (half + 1) * BANK],
+                in_=w_grouped[:, half * 4 * BANK : (half + 1) * 4 * BANK],
+            )
+
+        starts = [sum(GROUP_TILES[:g]) for g in range(len(GROUP_TILES))]
+        grouped_of = {}
+        codes_of = {}
+
+        def prepare_g(g):
+            count = GROUP_TILES[g]
+            grouped = ring.tile([P, 4 * BANK], BF16, name="grouped", tag="grouped", align_bytes=64)
+            for pair in range(count // 2):
+                a = starts[g] + 2 * pair
+                transpose_pair(
+                    (g_rows[a], g_rows[a + 1]),
+                    grouped[:].bitcast(F32)[:, pair * BANK : (pair + 1) * BANK],
+                    False,
+                )
+            grouped_of[g] = grouped
+
+        def quantise_g(g):
+            count = GROUP_TILES[g]
+            codes = ring.tile([P, BANK], U32, name="codes", tag="codes", align_bytes=64)
+            scales = ring.tile([P, BANK], U8, name="scales", tag="scales", align_bytes=64)
+            nc.vector.quantize_mx(
+                out=codes[:, : count * P].bitcast(E5M2X4),
+                scales=scales[:, : count * P],
+                in_=grouped_of[g][:, : count * K],
+            )
+            codes_of[g] = (codes, scales)
+
+        def multiply(g):
+            count = GROUP_TILES[g]
+            codes, scales = codes_of[g]
+            result = keep.tile([P, count, N], F32, name="result%d" % g)
+            for a in range(count):
+                for half in range(2):
+                    acc = psum.tile([P, BANK], F32, name="acc", tag="bank")
+                    nc.tensor.matmul_mx(
+                        out=acc[:],
+                        lhsT=codes[:, a * P : (a + 1) * P].bitcast(E5M2X4),
+                        lhsT_scale=scales[:, a * P : (a + 1) * P],
+                        rhs=w_codes[:, half * BANK : (half + 1) * BANK].bitcast(E4M3X4),
+                        rhs_scale=w_scales[:, half * BANK : (half + 1) * BANK],
+                        start=True,
+                        stop=True,
+                    )
+                    dst_ap = result[:, a, half * BANK : (half + 1) * BANK]
+                    if half == 0:
+                        nc.vector.tensor_copy(out=dst_ap, in_=acc[:])
+                    else:
+                        nc.scalar.copy(out=dst_ap, in_=acc[:])
+            nc.sync.dma_start(
+                out=out_dram[:, starts[g] : starts[g] + count, :], in_=result[:]
+            )
+
+        prepare_w(0)
+        prepare_g(0)
+        quantise_w(0)
+        prepare_w(1)
+        quantise_g(0)
+        quantise_w(1)
+        for g in range(len(GROUP_TILES)):
+            if g + 1 < len(GROUP_TILES):
+                prepare_g(g + 1)
+            multiply(g)
+            if g + 1 < len(GROUP_TILES):
+                quantise_g(g + 1)

@@ -28,7 +28,9 @@ HAMILTON = (
 )
 
 LOAD_TILES = (2, 2, 4, 8, 8, 8)
-GROUP_TILES = (2, 2, 4, 4, 4, 4, 4, 4, 4)
+GROUP_TILES = (2, 2, 2, 2, 2, 2, 4, 4, 4, 4, 4)
+PINNED = False
+WARM = 0
 
 
 def tile_qlinear_t_kernel(
@@ -36,6 +38,7 @@ def tile_qlinear_t_kernel(
 ):
     nc = tc.nc
     assert sum(LOAD_TILES) == TILES and sum(GROUP_TILES) == TILES
+    groups = len(GROUP_TILES)
     g_dram = grad_out.flatten_outer_dims().rearrange("(p a) k -> p a k", a=TILES)
     out_dram = out.flatten_outer_dims().rearrange("(p a) n -> p a n", a=TILES)
 
@@ -43,6 +46,8 @@ def tile_qlinear_t_kernel(
         keep = ctx.enter_context(tc.tile_pool(name="keep", bufs=1))
         ring = ctx.enter_context(tc.tile_pool(name="ring", bufs=3))
         psum = ctx.enter_context(tc.psum_pool(name="psum", bufs=8))
+        if PINNED:
+            ctx.enter_context(tc.manual_schedule())
 
         w_rows = [keep.tile([P, 2, K], BF16, name="w_rows%d" % rb) for rb in range(4)]
         for c, w in enumerate((r_weight, i_weight, j_weight, k_weight)):
@@ -61,7 +66,16 @@ def tile_qlinear_t_kernel(
         ident = keep.tile([P, P], F32, name="ident")
         masks.make_identity(nc, ident[:])
 
-        for rb in range(1, 4):
+        if WARM:
+            warm_in = keep.tile([P, BANK], BF16, name="warm_in")
+            nc.vector.memset(warm_in[:], 0.0)
+            warm_out = psum.tile([P, BANK], F32, name="warm_out", tag="bank")
+            for n in range(WARM):
+                nc.tensor.matmul(
+                    out=warm_out[:], lhsT=warm_in[:, :P], rhs=warm_in[:], start=True, stop=True
+                )
+
+        def sign_copies(rb):
             c = 0
             while c < 4:
                 src, sign = HAMILTON[rb][c]
@@ -94,24 +108,24 @@ def tile_qlinear_t_kernel(
         w_codes = keep.tile([P, N], U32, name="w_codes", align_bytes=64)
         w_scales = keep.tile([P, N], U8, name="w_scales", align_bytes=64)
 
-        def prepare_w(half):
-            for rb in (2 * half, 2 * half + 1):
-                transpose_pair(
-                    (w_rows[rb][:, 0, :], w_rows[rb][:, 1, :]),
-                    w_grouped[:].bitcast(F32)[:, rb * BANK : (rb + 1) * BANK],
-                    rb % 2 == 1,
-                )
-
-        def quantise_w(half):
-            nc.vector.quantize_mx(
-                out=w_codes[:, half * BANK : (half + 1) * BANK].bitcast(E4M3X4),
-                scales=w_scales[:, half * BANK : (half + 1) * BANK],
-                in_=w_grouped[:, half * 4 * BANK : (half + 1) * 4 * BANK],
+        def prepare_w(rb):
+            transpose_pair(
+                (w_rows[rb][:, 0, :], w_rows[rb][:, 1, :]),
+                w_grouped[:].bitcast(F32)[:, rb * BANK : (rb + 1) * BANK],
+                False,
             )
 
-        starts = [sum(GROUP_TILES[:g]) for g in range(len(GROUP_TILES))]
+        def quantise_w(rb):
+            nc.vector.quantize_mx(
+                out=w_codes[:, rb * 256 : (rb + 1) * 256].bitcast(E4M3X4),
+                scales=w_scales[:, rb * 256 : (rb + 1) * 256],
+                in_=w_grouped[:, rb * 1024 : (rb + 1) * 1024],
+            )
+
+        starts = [sum(GROUP_TILES[:g]) for g in range(groups)]
         grouped_of = {}
         codes_of = {}
+        result_of = {}
 
         def prepare_g(g):
             count = GROUP_TILES[g]
@@ -135,41 +149,65 @@ def tile_qlinear_t_kernel(
                 in_=grouped_of[g][:, : count * K],
             )
             codes_of[g] = (codes, scales)
+            result_of[g] = keep.tile([P, count, N], F32, name="result%d" % g)
 
-        def multiply(g):
-            count = GROUP_TILES[g]
+        def multiply(g, a, half, on_vector):
             codes, scales = codes_of[g]
-            result = keep.tile([P, count, N], F32, name="result%d" % g)
-            for a in range(count):
-                for half in range(2):
-                    acc = psum.tile([P, BANK], F32, name="acc", tag="bank")
-                    nc.tensor.matmul_mx(
-                        out=acc[:],
-                        lhsT=codes[:, a * P : (a + 1) * P].bitcast(E5M2X4),
-                        lhsT_scale=scales[:, a * P : (a + 1) * P],
-                        rhs=w_codes[:, half * BANK : (half + 1) * BANK].bitcast(E4M3X4),
-                        rhs_scale=w_scales[:, half * BANK : (half + 1) * BANK],
-                        start=True,
-                        stop=True,
-                    )
-                    dst_ap = result[:, a, half * BANK : (half + 1) * BANK]
-                    if half == 0:
-                        nc.vector.tensor_copy(out=dst_ap, in_=acc[:])
-                    else:
-                        nc.scalar.copy(out=dst_ap, in_=acc[:])
-            nc.sync.dma_start(
-                out=out_dram[:, starts[g] : starts[g] + count, :], in_=result[:]
+            acc = psum.tile([P, BANK], F32, name="acc", tag="bank")
+            nc.tensor.matmul_mx(
+                out=acc[:],
+                lhsT=codes[:, a * P : (a + 1) * P].bitcast(E5M2X4),
+                lhsT_scale=scales[:, a * P : (a + 1) * P],
+                rhs=w_codes[:, half * BANK : (half + 1) * BANK].bitcast(E4M3X4),
+                rhs_scale=w_scales[:, half * BANK : (half + 1) * BANK],
+                start=True,
+                stop=True,
             )
+            return acc
 
+        def evacuate(g, a, half, acc, on_vector):
+            dst_ap = result_of[g][:, a, half * BANK : (half + 1) * BANK]
+            if on_vector:
+                nc.vector.tensor_copy(out=dst_ap, in_=acc[:])
+            else:
+                nc.scalar.copy(out=dst_ap, in_=acc[:])
+
+        sign_copies(1)
         prepare_w(0)
-        prepare_g(0)
-        quantise_w(0)
+        sign_copies(2)
         prepare_w(1)
-        quantise_g(0)
+        quantise_w(0)
+        prepare_g(0)
+        sign_copies(3)
         quantise_w(1)
-        for g in range(len(GROUP_TILES)):
-            if g + 1 < len(GROUP_TILES):
+        prepare_w(2)
+        quantise_g(0)
+        prepare_w(3)
+        quantise_w(2)
+        for half in range(2):
+            accs = [multiply(0, a, half, True) for a in range(2)]
+            if half == 0:
+                quantise_w(3)
+            evacuate(0, 0, half, accs[0], True)
+            evacuate(0, 1, half, accs[1], False)
+            nc.sync.dma_start(
+                out=out_dram[:, 0:2, half * BANK : (half + 1) * BANK],
+                in_=result_of[0][:, :, half * BANK : (half + 1) * BANK],
+            )
+            if half == 0:
+                prepare_g(1)
+        quantise_g(1)
+
+        for g in range(1, groups):
+            count = GROUP_TILES[g]
+            if g + 1 < groups:
                 prepare_g(g + 1)
-            multiply(g)
-            if g + 1 < len(GROUP_TILES):
-                quantise_g(g + 1)
+            for a in range(count):
+                accs = [multiply(g, a, half, True) for half in range(2)]
+                evacuate(g, a, 0, accs[0], True)
+                evacuate(g, a, 1, accs[1], False)
+                if a == count // 2 - 1 and g + 1 < groups:
+                    quantise_g(g + 1)
+            nc.sync.dma_start(
+                out=out_dram[:, starts[g] : starts[g] + count, :], in_=result_of[g][:]
+            )

@@ -94,7 +94,7 @@ def tile_qlinear_t_kernel(
             bank = psum.tile([P, BANK], F32, name="bank", tag="bank")
             planes = bank[:].rearrange("p (a u j) -> p a u j", a=2, u=2)
             for a, rows in enumerate(rows_pair):
-                words = rows.bitcast(F32).rearrange("p (w u) -> p u w", u=2)
+                words = rows.bitcast(F32).rearrange("p (u w) -> p u w", u=2)
                 for u in range(2):
                     nc.tensor.transpose(planes[:, a, u, :], words[:, u, :], ident[:])
             dst_ap = grouped_words.rearrange("p (a j u) -> p a j u", a=2, u=2)

@@ -27,8 +27,9 @@ HAMILTON = (
     ((3, -1.0), (2, 1.0), (1, -1.0), (0, 1.0)),
 )
 
-LOAD_TILES = (2, 2, 4, 8, 8, 8)
-GROUP_TILES = (2, 2, 2, 2, 2, 2, 4, 4, 4, 4, 4)
+LOAD_TILES = (2, 6, 8, 16)
+GROUP_TILES = (2, 2, 4, 4, 4, 4, 4, 4, 4)
+STORE_TILES = (2, 2, 4, 4, 6, 6, 8)
 PINNED = False
 WARM = 0
 
@@ -37,7 +38,7 @@ def tile_qlinear_t_kernel(
     tc, x, r_weight, i_weight, j_weight, k_weight, bias, grad_out, out
 ):
     nc = tc.nc
-    assert sum(LOAD_TILES) == TILES and sum(GROUP_TILES) == TILES
+    assert sum(LOAD_TILES) == TILES and sum(GROUP_TILES) == TILES and sum(STORE_TILES) == TILES
     groups = len(GROUP_TILES)
     g_dram = grad_out.flatten_outer_dims().rearrange("(p a) k -> p a k", a=TILES)
     out_dram = out.flatten_outer_dims().rearrange("(p a) n -> p a n", a=TILES)
@@ -63,9 +64,6 @@ def tile_qlinear_t_kernel(
             g_rows.extend([chunk[:, a, :] for a in range(count)])
             first += count
 
-        ident = keep.tile([P, P], F32, name="ident")
-        masks.make_identity(nc, ident[:])
-
         if WARM:
             warm_in = keep.tile([P, BANK], BF16, name="warm_in")
             nc.vector.memset(warm_in[:], 0.0)
@@ -74,6 +72,9 @@ def tile_qlinear_t_kernel(
                 nc.tensor.matmul(
                     out=warm_out[:], lhsT=warm_in[:, :P], rhs=warm_in[:], start=True, stop=True
                 )
+
+        ident = keep.tile([P, P], F32, name="ident")
+        masks.make_identity(nc, ident[:])
 
         def sign_copies(rb):
             c = 0
@@ -125,7 +126,14 @@ def tile_qlinear_t_kernel(
         starts = [sum(GROUP_TILES[:g]) for g in range(groups)]
         grouped_of = {}
         codes_of = {}
+
         result_of = {}
+        first = 0
+        for s, count in enumerate(STORE_TILES):
+            result = keep.tile([P, count, N], F32, name="result%d" % s)
+            for a in range(count):
+                result_of[first + a] = (result, a, first, count)
+            first += count
 
         def prepare_g(g):
             count = GROUP_TILES[g]
@@ -149,9 +157,8 @@ def tile_qlinear_t_kernel(
                 in_=grouped_of[g][:, : count * K],
             )
             codes_of[g] = (codes, scales)
-            result_of[g] = keep.tile([P, count, N], F32, name="result%d" % g)
 
-        def multiply(g, a, half, on_vector):
+        def multiply(g, a, half):
             codes, scales = codes_of[g]
             acc = psum.tile([P, BANK], F32, name="acc", tag="bank")
             nc.tensor.matmul_mx(
@@ -166,11 +173,19 @@ def tile_qlinear_t_kernel(
             return acc
 
         def evacuate(g, a, half, acc, on_vector):
-            dst_ap = result_of[g][:, a, half * BANK : (half + 1) * BANK]
+            result, place, unused_first, unused_count = result_of[starts[g] + a]
+            dst_ap = result[:, place, half * BANK : (half + 1) * BANK]
             if on_vector:
                 nc.vector.tensor_copy(out=dst_ap, in_=acc[:])
             else:
                 nc.scalar.copy(out=dst_ap, in_=acc[:])
+
+        def store_if_full(g, a):
+            result, place, first_tile, count = result_of[starts[g] + a]
+            if place == count - 1:
+                nc.sync.dma_start(
+                    out=out_dram[:, first_tile : first_tile + count, :], in_=result[:]
+                )
 
         sign_copies(1)
         prepare_w(0)
@@ -185,17 +200,14 @@ def tile_qlinear_t_kernel(
         prepare_w(3)
         quantise_w(2)
         for half in range(2):
-            accs = [multiply(0, a, half, True) for a in range(2)]
+            accs = [multiply(0, a, half) for a in range(2)]
             if half == 0:
                 quantise_w(3)
             evacuate(0, 0, half, accs[0], True)
             evacuate(0, 1, half, accs[1], False)
-            nc.sync.dma_start(
-                out=out_dram[:, 0:2, half * BANK : (half + 1) * BANK],
-                in_=result_of[0][:, :, half * BANK : (half + 1) * BANK],
-            )
             if half == 0:
                 prepare_g(1)
+        store_if_full(0, 1)
         quantise_g(1)
 
         for g in range(1, groups):
@@ -203,11 +215,9 @@ def tile_qlinear_t_kernel(
             if g + 1 < groups:
                 prepare_g(g + 1)
             for a in range(count):
-                accs = [multiply(g, a, half, True) for half in range(2)]
+                accs = [multiply(g, a, half) for half in range(2)]
                 evacuate(g, a, 0, accs[0], True)
                 evacuate(g, a, 1, accs[1], False)
+                store_if_full(g, a)
                 if a == count // 2 - 1 and g + 1 < groups:
                     quantise_g(g + 1)
-            nc.sync.dma_start(
-                out=out_dram[:, starts[g] : starts[g] + count, :], in_=result_of[g][:]
-            )

@@ -31,7 +31,7 @@ LOAD_TILES = (2, 6, 8, 16)
 GROUP_TILES = (2, 2, 4, 4, 4, 4, 4, 4, 4)
 STORE_TILES = (2, 2, 4, 4, 6, 6, 8)
 PINNED = False
-WARM = 0
+WARM = 6
 
 
 def tile_qlinear_t_kernel(

@@ -20,16 +20,11 @@ BANK = 512
 FLOPS = 2 * TOKENS * K * N
 BYTES = TOKENS * K * 2 + 4 * 256 * 128 * 2 + TOKENS * N * 4
 
-HAMILTON = (
-    ((0, 1.0), (1, 1.0), (2, 1.0), (3, 1.0)),
-    ((1, -1.0), (0, 1.0), (3, 1.0), (2, -1.0)),
-    ((2, -1.0), (3, -1.0), (0, 1.0), (1, 1.0)),
-    ((3, -1.0), (2, 1.0), (1, -1.0), (0, 1.0)),
-)
+WINDOW = ((1, 4), (0, 5), (6, 1), (3, 0))
 
 LOAD_TILES = (2, 6, 8, 16)
 GROUP_TILES = (2, 2, 4, 4, 4, 4, 4, 4, 4)
-STORE_TILES = (2, 2, 4, 4, 6, 6, 8)
+STORE_TILES = (2, 2, 2, 2, 4, 4, 4, 4, 8)
 PINNED = False
 WARM = 6
 
@@ -50,10 +45,10 @@ def tile_qlinear_t_kernel(
         if PINNED:
             ctx.enter_context(tc.manual_schedule())
 
-        w_rows = [keep.tile([P, 2, K], BF16, name="w_rows%d" % rb) for rb in range(4)]
-        for c, w in enumerate((r_weight, i_weight, j_weight, k_weight)):
+        w_stage = keep.tile([P, 2, 8 * P], BF16, name="w_stage")
+        for block, w in ((1, r_weight), (2, i_weight), (4, j_weight), (5, k_weight)):
             nc.sync.dma_start(
-                out=w_rows[0][:, :, c * P : (c + 1) * P],
+                out=w_stage[:, :, block * P : (block + 1) * P],
                 in_=w.rearrange("(a p) k -> p a k", p=P),
             )
         g_rows = []
@@ -76,28 +71,21 @@ def tile_qlinear_t_kernel(
         ident = keep.tile([P, P], F32, name="ident")
         masks.make_identity(nc, ident[:])
 
-        def sign_copies(rb):
-            c = 0
-            while c < 4:
-                src, sign = HAMILTON[rb][c]
-                run = 1
-                while c + run < 4 and HAMILTON[rb][c + run] == (src + run, sign):
-                    run += 1
-                dst_ap = w_rows[rb][:, :, c * P : (c + run) * P]
-                src_ap = w_rows[0][:, :, src * P : (src + run) * P]
-                if sign > 0:
-                    nc.vector.tensor_copy(out=dst_ap, in_=src_ap)
-                else:
-                    nc.vector.tensor_scalar_mul(out=dst_ap, in0=src_ap, scalar1=-1.0)
-                c += run
+        def negate(dst, first, count):
+            nc.vector.tensor_scalar_mul(
+                out=w_stage[:, :, dst * P : (dst + count) * P],
+                in0=w_stage[:, :, first * P : (first + count) * P],
+                scalar1=-1.0,
+            )
 
-        def transpose_pair(rows_pair, grouped_words, on_vector):
+        def transpose_pair(rows_pair, windows, grouped_words, on_vector):
             bank = psum.tile([P, BANK], F32, name="bank", tag="bank")
             planes = bank[:].rearrange("p (a u j) -> p a u j", a=2, u=2)
             for a, rows in enumerate(rows_pair):
-                words = rows.bitcast(F32).rearrange("p (u w) -> p u w", u=2)
+                words = rows.bitcast(F32)
                 for u in range(2):
-                    nc.tensor.transpose(planes[:, a, u, :], words[:, u, :], ident[:])
+                    w0 = windows[u] * (P // 2)
+                    nc.tensor.transpose(planes[:, a, u, :], words[:, w0 : w0 + P], ident[:])
             dst_ap = grouped_words.rearrange("p (a j u) -> p a j u", a=2, u=2)
             src_ap = bank[:].rearrange("p (a u j) -> p a j u", a=2, u=2)
             if on_vector:
@@ -109,11 +97,12 @@ def tile_qlinear_t_kernel(
         w_codes = keep.tile([P, N], U32, name="w_codes", align_bytes=64)
         w_scales = keep.tile([P, N], U8, name="w_scales", align_bytes=64)
 
-        def prepare_w(rb):
+        def prepare_w(rb, on_vector):
             transpose_pair(
-                (w_rows[rb][:, 0, :], w_rows[rb][:, 1, :]),
+                (w_stage[:, 0, :], w_stage[:, 1, :]),
+                WINDOW[rb],
                 w_grouped[:].bitcast(F32)[:, rb * BANK : (rb + 1) * BANK],
-                False,
+                on_vector,
             )
 
         def quantise_w(rb):
@@ -142,6 +131,7 @@ def tile_qlinear_t_kernel(
                 a = starts[g] + 2 * pair
                 transpose_pair(
                     (g_rows[a], g_rows[a + 1]),
+                    (0, 2),
                     grouped[:].bitcast(F32)[:, pair * BANK : (pair + 1) * BANK],
                     False,
                 )
@@ -187,17 +177,17 @@ def tile_qlinear_t_kernel(
                     out=out_dram[:, first_tile : first_tile + count, :], in_=result[:]
                 )
 
-        sign_copies(1)
-        prepare_w(0)
-        sign_copies(2)
-        prepare_w(1)
-        quantise_w(0)
+        negate(0, 2, 1)
+        negate(6, 4, 2)
+        prepare_w(0, False)
+        prepare_w(1, True)
+        negate(3, 5, 1)
         prepare_g(0)
-        sign_copies(3)
+        quantise_w(0)
         quantise_w(1)
-        prepare_w(2)
+        prepare_w(2, False)
         quantise_g(0)
-        prepare_w(3)
+        prepare_w(3, False)
         quantise_w(2)
         for half in range(2):
             accs = [multiply(0, a, half) for a in range(2)]

@@ -45,12 +45,12 @@ def tile_qlinear_t_kernel(
         if PINNED:
             ctx.enter_context(tc.manual_schedule())
 
+        w_loaded = keep.tile([P, 4, 2 * P], BF16, name="w_loaded")
+        for c, w in enumerate((r_weight, i_weight, j_weight, k_weight)):
+            nc.sync.dma_start(out=w_loaded[:, c, :], in_=w.rearrange("(p a) k -> p (a k)", a=2))
         w_stage = keep.tile([P, 2, 8 * P], BF16, name="w_stage")
-        for block, w in ((1, r_weight), (2, i_weight), (4, j_weight), (5, k_weight)):
-            nc.sync.dma_start(
-                out=w_stage[:, :, block * P : (block + 1) * P],
-                in_=w.rearrange("(a p) k -> p a k", p=P),
-            )
+        staged = w_stage[:].rearrange("p a (b k) -> p a b k", k=P)
+        loaded = w_loaded[:].rearrange("p c (a k) -> p a c k", a=2)
         g_rows = []
         first = 0
         for c, count in enumerate(LOAD_TILES):
@@ -73,12 +73,12 @@ def tile_qlinear_t_kernel(
 
         def negate(dst, first, count):
             nc.vector.tensor_scalar_mul(
-                out=w_stage[:, :, dst * P : (dst + count) * P],
-                in0=w_stage[:, :, first * P : (first + count) * P],
+                out=staged[:, :, dst : dst + count, :],
+                in0=loaded[:, :, first : first + count, :],
                 scalar1=-1.0,
             )
 
-        def transpose_pair(rows_pair, windows, grouped_words, on_vector):
+        def transpose_pair(rows_pair, windows, grouped_words, on_vector, rows_interleaved=False):
             bank = psum.tile([P, BANK], F32, name="bank", tag="bank")
             planes = bank[:].rearrange("p (a u j) -> p a u j", a=2, u=2)
             for a, rows in enumerate(rows_pair):
@@ -86,8 +86,12 @@ def tile_qlinear_t_kernel(
                 for u in range(2):
                     w0 = windows[u] * (P // 2)
                     nc.tensor.transpose(planes[:, a, u, :], words[:, w0 : w0 + P], ident[:])
-            dst_ap = grouped_words.rearrange("p (a j u) -> p a j u", a=2, u=2)
-            src_ap = bank[:].rearrange("p (a u j) -> p a j u", a=2, u=2)
+            if rows_interleaved:
+                dst_ap = grouped_words.rearrange("p (j a u) -> p j a u", a=2, u=2)
+                src_ap = bank[:].rearrange("p (a u j) -> p j a u", a=2, u=2)
+            else:
+                dst_ap = grouped_words.rearrange("p (a j u) -> p a j u", a=2, u=2)
+                src_ap = bank[:].rearrange("p (a u j) -> p a j u", a=2, u=2)
             if on_vector:
                 nc.vector.tensor_copy(out=dst_ap, in_=src_ap)
             else:
@@ -103,6 +107,7 @@ def tile_qlinear_t_kernel(
                 WINDOW[rb],
                 w_grouped[:].bitcast(F32)[:, rb * BANK : (rb + 1) * BANK],
                 on_vector,
+                True,
             )
 
         def quantise_w(rb):
@@ -177,11 +182,13 @@ def tile_qlinear_t_kernel(
                     out=out_dram[:, first_tile : first_tile + count, :], in_=result[:]
                 )
 
-        negate(0, 2, 1)
-        negate(6, 4, 2)
+        nc.vector.tensor_copy(out=staged[:, :, 1:3, :], in_=loaded[:, :, 0:2, :])
+        nc.vector.tensor_copy(out=staged[:, :, 4:6, :], in_=loaded[:, :, 2:4, :])
+        negate(0, 1, 1)
+        negate(6, 2, 2)
         prepare_w(0, False)
         prepare_w(1, True)
-        negate(3, 5, 1)
+        negate(3, 3, 1)
         prepare_g(0)
         quantise_w(0)
         quantise_w(1)

@@ -22,9 +22,9 @@ BYTES = TOKENS * K * 2 + 4 * 256 * 128 * 2 + TOKENS * N * 4
 
 WINDOW = ((1, 4), (0, 5), (6, 1), (3, 0))
 
-LOAD_TILES = (2, 6, 8, 16)
+LOAD_TILES = (4, 12, 16)
 GROUP_TILES = (2, 2, 4, 4, 4, 4, 4, 4, 4)
-STORE_TILES = (2, 2, 2, 2, 4, 4, 4, 4, 8)
+STORE_TILES = (2, 2, 2, 3, 4, 5, 6, 8)
 PINNED = False
 WARM = 6
 

from contextlib import ExitStack

import concourse.masks as masks
import concourse.mybir as mybir

F32 = mybir.dt.float32
BF16 = mybir.dt.bfloat16
U32 = mybir.dt.uint32
U8 = mybir.dt.uint8
E4M3X4 = mybir.dt.float8_e4m3fn_x4
E5M2X4 = mybir.dt.float8_e5m2_x4

P = 128
TOKENS = 4096
K = 512
N = 1024
TILES = TOKENS // P
BANK = 512

FLOPS = 2 * TOKENS * K * N
BYTES = TOKENS * K * 2 + 4 * 256 * 128 * 2 + TOKENS * N * 4

WINDOW = ((1, 4), (0, 5), (6, 1), (3, 0))

LOAD_TILES = (4, 12, 16)
GROUP_TILES = (2, 2, 4, 4, 4, 4, 4, 4, 4)
STORE_TILES = (2, 2, 2, 3, 4, 5, 6, 8)
PINNED = False
WARM = 6


def tile_qlinear_t_kernel(
    tc, x, r_weight, i_weight, j_weight, k_weight, bias, grad_out, out
):
    nc = tc.nc
    assert sum(LOAD_TILES) == TILES and sum(GROUP_TILES) == TILES and sum(STORE_TILES) == TILES
    groups = len(GROUP_TILES)
    g_dram = grad_out.flatten_outer_dims().rearrange("(p a) k -> p a k", a=TILES)
    out_dram = out.flatten_outer_dims().rearrange("(p a) n -> p a n", a=TILES)

    with ExitStack() as ctx:
        keep = ctx.enter_context(tc.tile_pool(name="keep", bufs=1))
        ring = ctx.enter_context(tc.tile_pool(name="ring", bufs=3))
        psum = ctx.enter_context(tc.psum_pool(name="psum", bufs=8))
        if PINNED:
            ctx.enter_context(tc.manual_schedule())

        w_loaded = keep.tile([P, 4, 2 * P], BF16, name="w_loaded")
        for c, w in enumerate((r_weight, i_weight, j_weight, k_weight)):
            nc.sync.dma_start(out=w_loaded[:, c, :], in_=w.rearrange("(p a) k -> p (a k)", a=2))
        w_stage = keep.tile([P, 2, 8 * P], BF16, name="w_stage")
        staged = w_stage[:].rearrange("p a (b k) -> p a b k", k=P)
        loaded = w_loaded[:].rearrange("p c (a k) -> p a c k", a=2)
        g_rows = []
        first = 0
        for c, count in enumerate(LOAD_TILES):
            chunk = keep.tile([P, count, K], BF16, name="g_chunk%d" % c)
            nc.sync.dma_start(out=chunk[:], in_=g_dram[:, first : first + count, :])
            g_rows.extend([chunk[:, a, :] for a in range(count)])
            first += count

        if WARM:
            warm_in = keep.tile([P, BANK], BF16, name="warm_in")
            nc.vector.memset(warm_in[:], 0.0)
            warm_out = psum.tile([P, BANK], F32, name="warm_out", tag="bank")
            for n in range(WARM):
                nc.tensor.matmul(
                    out=warm_out[:], lhsT=warm_in[:, :P], rhs=warm_in[:], start=True, stop=True
                )

        ident = keep.tile([P, P], F32, name="ident")
        masks.make_identity(nc, ident[:])

        def negate(dst, first, count):
            nc.vector.tensor_scalar_mul(
                out=staged[:, :, dst : dst + count, :],
                in0=loaded[:, :, first : first + count, :],
                scalar1=-1.0,
            )

        def transpose_pair(rows_pair, windows, grouped_words, on_vector, rows_interleaved=False):
            bank = psum.tile([P, BANK], F32, name="bank", tag="bank")
            planes = bank[:].rearrange("p (a u j) -> p a u j", a=2, u=2)
            for a, rows in enumerate(rows_pair):
                words = rows.bitcast(F32)
                for u in range(2):
                    w0 = windows[u] * (P // 2)
                    nc.tensor.transpose(planes[:, a, u, :], words[:, w0 : w0 + P], ident[:])
            if rows_interleaved:
                dst_ap = grouped_words.rearrange("p (j a u) -> p j a u", a=2, u=2)
                src_ap = bank[:].rearrange("p (a u j) -> p j a u", a=2, u=2)
            else:
                dst_ap = grouped_words.rearrange("p (a j u) -> p a j u", a=2, u=2)
                src_ap = bank[:].rearrange("p (a u j) -> p a j u", a=2, u=2)
            if on_vector:
                nc.vector.tensor_copy(out=dst_ap, in_=src_ap)
            else:
                nc.scalar.copy(out=dst_ap, in_=src_ap)

        w_grouped = keep.tile([P, 4 * N], BF16, name="w_grouped", align_bytes=64)
        w_codes = keep.tile([P, N], U32, name="w_codes", align_bytes=64)
        w_scales = keep.tile([P, N], U8, name="w_scales", align_bytes=64)

        def prepare_w(rb, on_vector):
            transpose_pair(
                (w_stage[:, 0, :], w_stage[:, 1, :]),
                WINDOW[rb],
                w_grouped[:].bitcast(F32)[:, rb * BANK : (rb + 1) * BANK],
                on_vector,
                True,
            )

        def quantise_w(rb):
            nc.vector.quantize_mx(
                out=w_codes[:, rb * 256 : (rb + 1) * 256].bitcast(E4M3X4),
                scales=w_scales[:, rb * 256 : (rb + 1) * 256],
                in_=w_grouped[:, rb * 1024 : (rb + 1) * 1024],
            )

        starts = [sum(GROUP_TILES[:g]) for g in range(groups)]
        grouped_of = {}
        codes_of = {}

        result_of = {}
        first = 0
        for s, count in enumerate(STORE_TILES):
            result = keep.tile([P, count, N], F32, name="result%d" % s)
            for a in range(count):
                result_of[first + a] = (result, a, first, count)
            first += count

        def prepare_g(g):
            count = GROUP_TILES[g]
            grouped = ring.tile([P, 4 * BANK], BF16, name="grouped", tag="grouped", align_bytes=64)
            for pair in range(count // 2):
                a = starts[g] + 2 * pair
                transpose_pair(
                    (g_rows[a], g_rows[a + 1]),
                    (0, 2),
                    grouped[:].bitcast(F32)[:, pair * BANK : (pair + 1) * BANK],
                    False,
                )
            grouped_of[g] = grouped

        def quantise_g(g):
            count = GROUP_TILES[g]
            codes = ring.tile([P, BANK], U32, name="codes", tag="codes", align_bytes=64)
            scales = ring.tile([P, BANK], U8, name="scales", tag="scales", align_bytes=64)
            nc.vector.quantize_mx(
                out=codes[:, : count * P].bitcast(E5M2X4),
                scales=scales[:, : count * P],
                in_=grouped_of[g][:, : count * K],
            )
            codes_of[g] = (codes, scales)

        def multiply(g, a, half):
            codes, scales = codes_of[g]
            acc = psum.tile([P, BANK], F32, name="acc", tag="bank")
            nc.tensor.matmul_mx(
                out=acc[:],
                lhsT=codes[:, a * P : (a + 1) * P].bitcast(E5M2X4),
                lhsT_scale=scales[:, a * P : (a + 1) * P],
                rhs=w_codes[:, half * BANK : (half + 1) * BANK].bitcast(E4M3X4),
                rhs_scale=w_scales[:, half * BANK : (half + 1) * BANK],
                start=True,
                stop=True,
            )
            return acc

        def evacuate(g, a, half, acc, on_vector):
            result, place, unused_first, unused_count = result_of[starts[g] + a]
            dst_ap = result[:, place, half * BANK : (half + 1) * BANK]
            if on_vector:
                nc.vector.tensor_copy(out=dst_ap, in_=acc[:])
            else:
                nc.scalar.copy(out=dst_ap, in_=acc[:])

        def store_if_full(g, a):
            result, place, first_tile, count = result_of[starts[g] + a]
            if place == count - 1:
                nc.sync.dma_start(
                    out=out_dram[:, first_tile : first_tile + count, :], in_=result[:]
                )

        nc.vector.tensor_copy(out=staged[:, :, 1:3, :], in_=loaded[:, :, 0:2, :])
        nc.vector.tensor_copy(out=staged[:, :, 4:6, :], in_=loaded[:, :, 2:4, :])
        negate(0, 1, 1)
        negate(6, 2, 2)
        prepare_w(0, False)
        prepare_w(1, True)
        negate(3, 3, 1)
        prepare_g(0)
        quantise_w(0)
        quantise_w(1)
        prepare_w(2, False)
        quantise_g(0)
        prepare_w(3, False)
        quantise_w(2)
        for half in range(2):
            accs = [multiply(0, a, half) for a in range(2)]
            if half == 0:
                quantise_w(3)
            evacuate(0, 0, half, accs[0], True)
            evacuate(0, 1, half, accs[1], False)
            if half == 0:
                prepare_g(1)
        store_if_full(0, 1)
        quantise_g(1)

        for g in range(1, groups):
            count = GROUP_TILES[g]
            if g + 1 < groups:
                prepare_g(g + 1)
            for a in range(count):
                accs = [multiply(g, a, half) for half in range(2)]
                evacuate(g, a, 0, accs[0], True)
                evacuate(g, a, 1, accs[1], False)
                store_if_full(g, a)
                if a == count // 2 - 1 and g + 1 < groups:
                    quantise_g(g + 1)
